import numpy as np
import ml_dtypes

BF16 = ml_dtypes.bfloat16


def bf(x):
    return np.asarray(x, np.float32).astype(BF16)


def f32(x):
    return np.asarray(x, np.float32)


def f64(x):
    return np.asarray(x).astype(np.float64)


def striped(idx):
    return np.tile(idx.reshape(-1, 16).T, (8, 1))


C, S, N, NPAIR = 512, 256, 512, 255


def positional():
    pos = np.arange(N, dtype=np.float32)[None, :]
    pair = np.arange(NPAIR, dtype=np.float32)[:, None]
    angle = pos / np.power(np.float32(10000.0), np.float32(2.0) * pair / np.float32(C))
    pe = np.zeros((C, N), np.float32)
    pe[0:2 * NPAIR:2] = np.sin(angle)
    pe[1:2 * NPAIR:2] = np.cos(angle)
    return pe


def setup_inputs():
    return {"table": f32(np.random.standard_normal((C, S))), "pe": f32(positional()), "offs": striped(np.random.permutation(np.tile(np.arange(S), 2))[:N])}


def reference(table, pe, offs):
    idx = offs[:16].T.reshape(-1)
    return f64(table)[:, idx] + f64(pe)

@@ -1,0 +1,38 @@
+import concourse.mybir as mybir
+
+F32 = mybir.dt.float32
+U16 = mybir.dt.uint16
+ADD = mybir.AluOpType.add
+
+P = 128
+C = 512
+S = 256
+N = 512
+PIECE = S
+PER_COLUMN = 16
+
+
+def tile_embedding_kernel(tc, table, pe, offs, out):
+    nc = tc.nc
+    n_blocks = C // P
+    with (
+        tc.tile_pool(name="held", bufs=1) as held,
+        tc.tile_pool(name="blocks", bufs=n_blocks) as blocks,
+    ):
+        offsets = held.tile([P, N // PER_COLUMN], U16, name="offsets")
+        nc.sync.dma_start(offsets[:], offs)
+
+        for b in range(n_blocks):
+            rows = slice(b * P, (b + 1) * P)
+            words = blocks.tile([P, S], F32, name="words")
+            places = blocks.tile([P, N], F32, name="places")
+            summed = blocks.tile([P, N], F32, name="summed")
+            nc.sync.dma_start(words[:], table[rows, :])
+            nc.scalar.dma_start(places[:], pe[rows, :])
+
+            for k in range(N // PIECE):
+                cols = slice(k * PIECE, (k + 1) * PIECE)
+                piece = offsets[:, k * PIECE // PER_COLUMN : (k + 1) * PIECE // PER_COLUMN]
+                nc.vector.tensor_tensor(summed[:, cols], words[:].indirect(piece), places[:, cols], ADD)
+
+            nc.sync.dma_start(out[rows, :], summed[:])

@@ -34,5 +34,4 @@ def tile_embedding_kernel(tc, table, pe, offs, out):
                 cols = slice(k * PIECE, (k + 1) * PIECE)
                 piece = offsets[:, k * PIECE // PER_COLUMN : (k + 1) * PIECE // PER_COLUMN]
                 nc.vector.tensor_tensor(summed[:, cols], words[:].indirect(piece), places[:, cols], ADD)
-
-            nc.sync.dma_start(out[rows, :], summed[:])
+                nc.sync.dma_start(out[rows, cols], summed[:, cols])

@@ -11,27 +11,42 @@ N = 512
 PIECE = S
 PER_COLUMN = 16
 
+N_BLOCKS = C // P
+N_PIECES = N // PIECE
+
 
 def tile_embedding_kernel(tc, table, pe, offs, out):
     nc = tc.nc
-    n_blocks = C // P
     with (
         tc.tile_pool(name="held", bufs=1) as held,
-        tc.tile_pool(name="blocks", bufs=n_blocks) as blocks,
+        tc.tile_pool(name="blocks", bufs=N_BLOCKS) as blocks,
+        tc.tile_pool(name="pieces", bufs=N_BLOCKS * N_PIECES) as pieces,
     ):
         offsets = held.tile([P, N // PER_COLUMN], U16, name="offsets")
         nc.sync.dma_start(offsets[:], offs)
 
-        for b in range(n_blocks):
+        queues = (nc.scalar, nc.sync)
+        n_loads = 0
+        words = []
+        places = []
+        for b in range(N_BLOCKS):
             rows = slice(b * P, (b + 1) * P)
-            words = blocks.tile([P, S], F32, name="words")
-            places = blocks.tile([P, N], F32, name="places")
-            summed = blocks.tile([P, N], F32, name="summed")
-            nc.sync.dma_start(words[:], table[rows, :])
-            nc.scalar.dma_start(places[:], pe[rows, :])
+            words.append(blocks.tile([P, S], F32, name="words"))
+            queues[n_loads % 2].dma_start(words[b][:], table[rows, :])
+            n_loads += 1
+            for k in range(N_PIECES):
+                cols = slice(k * PIECE, (k + 1) * PIECE)
+                places.append(pieces.tile([P, PIECE], F32, name="places"))
+                queues[n_loads % 2].dma_start(places[b * N_PIECES + k][:], pe[rows, cols])
+                n_loads += 1
 
-            for k in range(N // PIECE):
+        for b in range(N_BLOCKS):
+            rows = slice(b * P, (b + 1) * P)
+            for k in range(N_PIECES):
                 cols = slice(k * PIECE, (k + 1) * PIECE)
                 piece = offsets[:, k * PIECE // PER_COLUMN : (k + 1) * PIECE // PER_COLUMN]
-                nc.vector.tensor_tensor(summed[:, cols], words[:].indirect(piece), places[:, cols], ADD)
-                nc.sync.dma_start(out[rows, cols], summed[:, cols])
+                summed = pieces.tile([P, PIECE], F32, name="summed")
+                nc.vector.tensor_tensor(
+                    summed[:], words[b][:].indirect(piece), places[b * N_PIECES + k][:], ADD
+                )
+                nc.sync.dma_start(out[rows, cols], summed[:])

@@ -20,7 +20,6 @@ def tile_embedding_kernel(tc, table, pe, offs, out):
     with (
         tc.tile_pool(name="held", bufs=1) as held,
         tc.tile_pool(name="blocks", bufs=N_BLOCKS) as blocks,
-        tc.tile_pool(name="pieces", bufs=N_BLOCKS * N_PIECES) as pieces,
     ):
         offsets = held.tile([P, N // PER_COLUMN], U16, name="offsets")
         nc.sync.dma_start(offsets[:], offs)
@@ -34,19 +33,25 @@ def tile_embedding_kernel(tc, table, pe, offs, out):
             words.append(blocks.tile([P, S], F32, name="words"))
             queues[n_loads % 2].dma_start(words[b][:], table[rows, :])
             n_loads += 1
-            for k in range(N_PIECES):
-                cols = slice(k * PIECE, (k + 1) * PIECE)
-                places.append(pieces.tile([P, PIECE], F32, name="places"))
-                queues[n_loads % 2].dma_start(places[b * N_PIECES + k][:], pe[rows, cols])
+            places.append(blocks.tile([P, N], F32, name="places"))
+            widths = [PIECE] * N_PIECES if b == 0 else [N]
+            start = 0
+            for width in widths:
+                cols = slice(start, start + width)
+                queues[n_loads % 2].dma_start(places[b][:, cols], pe[rows, cols])
                 n_loads += 1
+                start += width
 
         for b in range(N_BLOCKS):
             rows = slice(b * P, (b + 1) * P)
+            summed = blocks.tile([P, N], F32, name="summed")
             for k in range(N_PIECES):
                 cols = slice(k * PIECE, (k + 1) * PIECE)
                 piece = offsets[:, k * PIECE // PER_COLUMN : (k + 1) * PIECE // PER_COLUMN]
-                summed = pieces.tile([P, PIECE], F32, name="summed")
                 nc.vector.tensor_tensor(
-                    summed[:], words[b][:].indirect(piece), places[b * N_PIECES + k][:], ADD
+                    summed[:, cols], words[b][:].indirect(piece), places[b][:, cols], ADD
                 )
-                nc.sync.dma_start(out[rows, cols], summed[:])
+                if b == N_BLOCKS - 1:
+                    nc.sync.dma_start(out[rows, cols], summed[:, cols])
+            if b < N_BLOCKS - 1:
+                nc.sync.dma_start(out[rows, :], summed[:])

@@ -22,7 +22,6 @@ def tile_embedding_kernel(tc, table, pe, offs, out):
         tc.tile_pool(name="blocks", bufs=N_BLOCKS) as blocks,
     ):
         offsets = held.tile([P, N // PER_COLUMN], U16, name="offsets")
-        nc.sync.dma_start(offsets[:], offs)
 
         queues = (nc.scalar, nc.sync)
         n_loads = 0
@@ -40,6 +39,8 @@ def tile_embedding_kernel(tc, table, pe, offs, out):
                 cols = slice(start, start + width)
                 queues[n_loads % 2].dma_start(places[b][:, cols], pe[rows, cols])
                 n_loads += 1
+                if b == 0 and start == 0:
+                    nc.sync.dma_start(offsets[:], offs)
                 start += width
 
         for b in range(N_BLOCKS):

@@ -43,6 +43,11 @@ def tile_embedding_kernel(tc, table, pe, offs, out):
                     nc.sync.dma_start(offsets[:], offs)
                 start += width
 
+        zeros = held.tile([P, PER_COLUMN], F32, name="zeros")
+        nc.vector.memset(zeros[:], 0.0)
+        warm = held.tile([P, PER_COLUMN], F32, name="warm")
+        nc.vector.tensor_tensor(warm[:], zeros[:], zeros[:], ADD)
+
         for b in range(N_BLOCKS):
             rows = slice(b * P, (b + 1) * P)
             summed = blocks.tile([P, N], F32, name="summed")

import concourse.mybir as mybir

F32 = mybir.dt.float32
U16 = mybir.dt.uint16
ADD = mybir.AluOpType.add

P = 128
C = 512
S = 256
N = 512
PIECE = S
PER_COLUMN = 16

N_BLOCKS = C // P
N_PIECES = N // PIECE


def tile_embedding_kernel(tc, table, pe, offs, out):
    nc = tc.nc
    with (
        tc.tile_pool(name="held", bufs=1) as held,
        tc.tile_pool(name="blocks", bufs=N_BLOCKS) as blocks,
    ):
        offsets = held.tile([P, N // PER_COLUMN], U16, name="offsets")

        queues = (nc.scalar, nc.sync)
        n_loads = 0
        words = []
        places = []
        for b in range(N_BLOCKS):
            rows = slice(b * P, (b + 1) * P)
            words.append(blocks.tile([P, S], F32, name="words"))
            queues[n_loads % 2].dma_start(words[b][:], table[rows, :])
            n_loads += 1
            places.append(blocks.tile([P, N], F32, name="places"))
            widths = [PIECE] * N_PIECES if b == 0 else [N]
            start = 0
            for width in widths:
                cols = slice(start, start + width)
                queues[n_loads % 2].dma_start(places[b][:, cols], pe[rows, cols])
                n_loads += 1
                if b == 0 and start == 0:
                    nc.sync.dma_start(offsets[:], offs)
                start += width

        zeros = held.tile([P, PER_COLUMN], F32, name="zeros")
        nc.vector.memset(zeros[:], 0.0)
        warm = held.tile([P, PER_COLUMN], F32, name="warm")
        nc.vector.tensor_tensor(warm[:], zeros[:], zeros[:], ADD)

        for b in range(N_BLOCKS):
            rows = slice(b * P, (b + 1) * P)
            summed = blocks.tile([P, N], F32, name="summed")
            for k in range(N_PIECES):
                cols = slice(k * PIECE, (k + 1) * PIECE)
                piece = offsets[:, k * PIECE // PER_COLUMN : (k + 1) * PIECE // PER_COLUMN]
                nc.vector.tensor_tensor(
                    summed[:, cols], words[b][:].indirect(piece), places[b][:, cols], ADD
                )
                if b == N_BLOCKS - 1:
                    nc.sync.dma_start(out[rows, cols], summed[:, cols])
            if b < N_BLOCKS - 1:
                nc.sync.dma_start(out[rows, :], summed[:])
